import numpy as np
import ml_dtypes


def mxq(x, axis, fmt="e4m3"):
    dtype, down = {"e4m3": (ml_dtypes.float8_e4m3fn, 7), "e5m2": (ml_dtypes.float8_e5m2, 14)}[fmt]
    v = np.moveaxis(np.asarray(x, np.float32).astype(ml_dtypes.bfloat16).astype(np.float64), axis, -1)
    blocks = v.reshape(v.shape[:-1] + (-1, 32))
    amax = np.abs(blocks).max(-1, keepdims=True)
    byte = np.maximum(np.where(amax > 0, np.frexp(amax)[1] - 1 + 127, 0) - down, 1)
    scale = np.exp2(byte - 127.0)
    codes = (blocks / scale).astype(np.float32).astype(dtype).astype(np.float64)
    return np.moveaxis((codes * scale).reshape(v.shape), -1, axis)


WIDE = False


def mx_kscale(k):
    if not WIDE:
        return np.ones(k)
    levels = np.array([10, -10, 5, -5, 0])
    if k % 512:
        return np.exp2(np.random.permutation(np.resize(levels, k // 32))).repeat(32)
    a = np.empty((k // 512, 16))
    for p in range(k // 512):
        a[p, :8] = np.random.permutation(np.resize(levels, 8))
        for g in range(8):
            far = levels[np.abs(levels - a[p, g]) >= 10]
            a[p, g + 8] = far[np.random.randint(len(far))]
    return np.exp2(a.ravel()).repeat(32)


BF16 = ml_dtypes.bfloat16


def bf(x):
    return np.asarray(x, np.float32).astype(BF16)


def f64(x):
    return np.asarray(x).astype(np.float64)


B, W, U, H, D, K, MAX_BACK, MAX_FWD = 2, 8, 256, 1, 1024, 512, 255, 0
CH = H * D
F = MAX_BACK + MAX_FWD + 1


def setup_inputs():
    s, t = mx_kscale(CH), mx_kscale(D)
    a = 1.5 * D ** -0.25
    return {"queries": bf(np.random.standard_normal((B, W, U, H, D)) * a * t),
            "keys": bf(np.random.standard_normal((B, W, K, H, D)) * a / t),
            "sin_emb": bf(np.random.standard_normal((F, CH)) * np.sqrt(0.5) * s),
            "pos_w": bf(np.random.standard_normal((CH, CH)) * 2.0 * D ** -0.25 / np.sqrt(CH) / s[None, :] / np.tile(t, H)[:, None])}


def relative_shift(x):
    pad = K + 1 - F
    x = np.pad(x, ((0, 0), (0, 0), (0, 0), (0, 0), (0, pad)))
    x = x.reshape(B, H, W, U * (K + 1))[:, :, :, : U * K]
    return x.reshape(B, H, W, U, K)


def reference(queries, keys, sin_emb, pos_w):
    proj = (mxq(f64(sin_emb), 1, "e4m3") @ mxq(f64(pos_w), 1, "e4m3").T).reshape(F, H, D)
    qq = mxq(f64(queries), 4, "e4m3").transpose(0, 3, 1, 2, 4)
    kq = mxq(f64(keys), 4, "e4m3").transpose(0, 3, 1, 4, 2)
    pq = mxq(proj, 2, "e4m3").transpose(1, 2, 0)[None, :, None]
    term_ac = qq @ kq
    term_bd = qq @ pq
    return term_ac + relative_shift(term_bd)

@@ -1,0 +1,311 @@
+from contextlib import ExitStack
+
+import concourse.mybir as mybir
+from concourse.masks import make_identity
+
+F32 = mybir.dt.float32
+BF16 = mybir.dt.bfloat16
+U32 = mybir.dt.uint32
+U8 = mybir.dt.uint8
+FP8X4 = mybir.dt.float8_e4m3fn_x4
+ADD = mybir.AluOpType.add
+IS_GE = mybir.AluOpType.is_ge
+
+P = 128
+NBLK = 16
+U = 256
+C = 512
+D = 1024
+F = 256
+PITCH = 128 + 2 * F
+Q_AHEAD = 8
+B_AHEAD = 4
+K_LOAD = 2
+Q_LOAD = Q_AHEAD + 2
+STORE_LAG = 7
+EARLY_K_LOADS = {-6: 0, -5: 1, -3: 2, -1: 3}
+
+FLOPS = 2 * F * D * D + NBLK * 2 * U * D * (C + F)
+
+
+def tile_gemma3naudiorelativepositionembedding_pa_t_kernel(tc, queries, keys, sin_emb, pos_w, out):
+    nc = tc.nc
+    q_view = queries.rearrange("b w (p e) h d -> (b w) p (e h d)", e=2)
+    k_view = keys.rearrange("b w (p t) h d -> (b w) p (t h d)", t=4)
+    s_view = sin_emb.rearrange("(p e) i -> p (e i)", e=2)
+    w_view = pos_w.rearrange("(g p t e) i -> g t p (e i)", g=2, t=2, e=2)
+    o_view = out.rearrange("b h w (t p) c -> (b h w) p t c", t=2)
+    o_flat = out.rearrange("b h w u c -> (b h w) (u c)")
+
+    with ExitStack() as ctx:
+        const = ctx.enter_context(tc.tile_pool(name="const", bufs=1))
+        raws = ctx.enter_context(tc.tile_pool(name="raws", bufs=6))
+        work = ctx.enter_context(tc.tile_pool(name="work", bufs=2))
+        keep = ctx.enter_context(tc.tile_pool(name="keep", bufs=Q_AHEAD + 3))
+        psum = ctx.enter_context(tc.psum_pool(name="psum", bufs=2))
+        ctx.enter_context(tc.manual_schedule())
+
+        pair_raw = {}
+        k_raw = {}
+        pair_grouped = {}
+        q_mx = {}
+        k_grouped = {}
+        k_mx = {}
+        accs = {}
+        bds = {}
+        parks = {}
+        shifted = {}
+        results = {}
+
+        def load_pair_rows(key, src):
+            raw = raws.tile([P, 2 * D], BF16, tag="qraw", bufs=8)
+            nc.sync.dma_start(out=raw[:], in_=src)
+            pair_raw[key] = raw
+
+        def load_k(i):
+            raw = raws.tile([P, 4 * D], BF16, tag="kraw", bufs=4)
+            nc.sync.dma_start(out=raw[:], in_=k_view[i])
+            k_raw[i] = raw
+
+        load_pair_rows("s", s_view)
+        for h in range(4):
+            load_pair_rows("w%d" % h, w_view[h // 2, h % 2])
+        for n in range(2):
+            load_pair_rows(n, q_view[n])
+
+        ident = const.tile([P, P], F32, name="ident")
+        make_identity(nc, ident[:])
+        lows = []
+        for n in range(B_AHEAD + 2):
+            low = const.tile([P, 4, 128], F32, name="low%d" % n)
+            nc.gpsimd.memset(low[:], 0.0)
+            lows.append(low)
+
+        def copy_out(engine, dst, src):
+            if engine == 0:
+                nc.scalar.copy(out=dst, in_=src)
+            else:
+                nc.vector.tensor_copy(out=dst, in_=src)
+
+        def transpose_pair_rows(key, natural, engines):
+            words = pair_raw[key][:].bitcast(F32)
+            grouped = work.tile([P, 2 * U * 4], BF16, tag="qg", bufs=3, align_bytes=64)
+            g32 = grouped[:].bitcast(F32).rearrange("p (g c u) -> p g c u", g=2, u=2)
+            for g in range(2):
+                bank = psum.tile([P, 4, P], F32, tag="tp", bufs=4)
+                for e in range(2):
+                    for u2 in range(2):
+                        col = 512 * e + 256 * g
+                        nc.tensor.transpose(bank[:, 2 * e + u2, :], words[:, col + u2 : col + 256 : 2], ident[:])
+                if natural:
+                    dst = g32[:, g].rearrange("p (r e) u -> p r e u", e=2)
+                    bsrc = bank[:].rearrange("p (e u) r -> p r e u", e=2)
+                else:
+                    dst = g32[:, g].rearrange("p (e r) u -> p e r u", e=2)
+                    bsrc = bank[:].rearrange("p (e u) r -> p e r u", e=2)
+                copy_out(engines[g], dst, bsrc)
+            pair_grouped[key] = grouped
+
+        def quantise_pair_rows(key, codes, scales):
+            nc.vector.quantize_mx(out=codes.bitcast(FP8X4), scales=scales, in_=pair_grouped[key][:])
+
+        s_codes = const.tile([P, 2 * F], U32, name="s_codes", align_bytes=64)
+        s_scales = const.tile([P, 2 * F], U8, name="s_scales", align_bytes=64)
+        w_codes = const.tile([P, 4, 512], U32, name="w_codes", align_bytes=64)
+        w_scales = const.tile([P, 4, 512], U8, name="w_scales", align_bytes=64)
+        p_grouped = const.tile([P, 2 * F * 4], BF16, name="p_grouped", align_bytes=64)
+        pg = p_grouped[:].rearrange("p (g f t) -> p g f t", g=2, t=4)
+        p_codes = const.tile([P, 2 * F], U32, name="p_codes", align_bytes=64)
+        p_scales = const.tile([P, 2 * F], U8, name="p_scales", align_bytes=64)
+
+        transpose_pair_rows("s", True, (0, 1))
+        transpose_pair_rows("w0", False, (0, 1))
+        quantise_pair_rows("s", s_codes[:], s_scales[:])
+        for h in range(1, 4):
+            transpose_pair_rows("w%d" % h, False, (0, 1))
+            quantise_pair_rows("w%d" % (h - 1), w_codes[:, h - 1, :], w_scales[:, h - 1, :])
+
+        def project():
+            quantise_pair_rows("w3", w_codes[:, 3, :], w_scales[:, 3, :])
+            for g in range(2):
+                for fh in range(2):
+                    pb = psum.tile([P, 4, 128], F32, tag="bd", bufs=2)
+                    for t in range(4):
+                        h = 2 * g + t // 2
+                        e = t % 2
+                        for gi in range(2):
+                            wcol = 256 * gi + 128 * e
+                            scol = 256 * gi + 128 * fh
+                            nc.tensor.matmul_mx(
+                                out=pb[:, t, :],
+                                lhsT=w_codes[:, h, wcol : wcol + 128].bitcast(FP8X4),
+                                lhsT_scale=w_scales[:, h, wcol : wcol + 128],
+                                rhs=s_codes[:, scol : scol + 128].bitcast(FP8X4),
+                                rhs_scale=s_scales[:, scol : scol + 128],
+                                start=(gi == 0),
+                                stop=(gi == 1),
+                            )
+                    copy_out(fh, pg[:, g, 128 * fh : 128 * fh + 128, :], pb[:].rearrange("p t f -> p f t"))
+            nc.vector.quantize_mx(out=p_codes[:].bitcast(FP8X4), scales=p_scales[:], in_=p_grouped[:])
+
+        def quantise_q(j):
+            q_codes = keep.tile([P, 2 * U], U32, tag="q_codes", align_bytes=64)
+            q_scales = keep.tile([P, 2 * U], U8, tag="q_scales", align_bytes=64)
+            quantise_pair_rows(j, q_codes[:], q_scales[:])
+            q_mx[j] = (q_codes, q_scales)
+
+        def positions(j, t):
+            q_codes, q_scales = q_mx[j]
+            if t == 0:
+                bds[j] = psum.tile([P, 2, F], F32, tag="bd", bufs=2, name="bd")
+            bd = bds[j]
+            for g in range(2):
+                qcol = 256 * g + 128 * t
+                nc.tensor.matmul_mx(
+                    out=bd[:, t, :],
+                    lhsT=q_codes[:, qcol : qcol + 128].bitcast(FP8X4),
+                    lhsT_scale=q_scales[:, qcol : qcol + 128],
+                    rhs=p_codes[:, 256 * g : 256 * g + 256].bitcast(FP8X4),
+                    rhs_scale=p_scales[:, 256 * g : 256 * g + 256],
+                    start=(g == 0),
+                    stop=(g == 1),
+                )
+
+        def park_rows(j):
+            bd = bds[j]
+            park = work.tile([P, PITCH], F32, tag="park", bufs=3)
+            nc.scalar.copy(out=park[:, 128:PITCH], in_=bd[:].rearrange("p t f -> p (t f)"))
+            nc.scalar.copy(out=park[:, 0:128], in_=bd[:, 1, 128:256])
+            parks[j] = park
+
+        def park_write(j):
+            nc.sync.dma_start(
+                out=o_flat[j, 0 : P * PITCH].rearrange("(p s) -> p s", s=PITCH), in_=parks[j][:]
+            )
+
+        def read_back(j):
+            x = keep.tile([P, 4, 128], F32, tag="x", bufs=B_AHEAD + 2)
+            nc.sync.dma_start(
+                out=x[:].rearrange("p s j -> p (s j)"),
+                in_=o_flat[j, 128 : 128 + P * (PITCH - 1)].rearrange("(p s) -> p s", s=PITCH - 1)[:, 0:512],
+            )
+            low = lows[j % (B_AHEAD + 2)]
+            for n in range(2):
+                shared = x[:, 2 * n, :]
+                nc.gpsimd.affine_select(
+                    out=low[:, 1 + n, :], in_=shared, pattern=[[-1, 128]],
+                    compare_op=IS_GE, fill=0.0, base=-1, channel_multiplier=1,
+                )
+                nc.gpsimd.affine_select(
+                    out=shared, in_=shared, pattern=[[1, 128]],
+                    compare_op=IS_GE, fill=0.0, base=0, channel_multiplier=-1,
+                )
+            shifted[j] = (x, low)
+
+        def transpose_k(i, banks):
+            words = k_raw[i][:].bitcast(F32)
+            if banks[0] == 0:
+                k_grouped[i] = work.tile([P, 2 * C * 4], BF16, tag="kg", align_bytes=64, name="kg")
+            grouped = k_grouped[i]
+            g32 = grouped[:].bitcast(F32).rearrange("p (g n u) -> p g n u", g=2, u=2)
+            for tt in banks:
+                bank = psum.tile([P, 4, P], F32, tag="tp", bufs=4)
+                for w in range(4):
+                    col = 512 * tt + 256 * (w // 2)
+                    nc.tensor.transpose(bank[:, w, :], words[:, col + w % 2 : col + 256 : 2], ident[:])
+                copy_out(
+                    1 if tt == 3 else 0,
+                    g32[:, :, 128 * tt : 128 * tt + 128, :],
+                    bank[:].rearrange("p (g u) r -> p g r u", g=2),
+                )
+
+        def quantise_k(i):
+            k_codes = work.tile([P, 2 * C], U32, tag="k_codes", align_bytes=64)
+            k_scales = work.tile([P, 2 * C], U8, tag="k_scales", align_bytes=64)
+            nc.vector.quantize_mx(out=k_codes[:].bitcast(FP8X4), scales=k_scales[:], in_=k_grouped[i][:])
+            k_mx[i] = (k_codes, k_scales)
+
+        def content(i, t):
+            q_codes, q_scales = q_mx[i]
+            k_codes, k_scales = k_mx[i]
+            acc = psum.tile([P, C], F32, tag="ac", bufs=2)
+            for g in (-1, 0, 1):
+                lone = g < 0
+                g = max(g, 0)
+                qcol = 256 * g + 128 * t
+                nc.tensor.matmul_mx(
+                    out=acc[:],
+                    lhsT=q_codes[:, qcol : qcol + 128].bitcast(FP8X4),
+                    lhsT_scale=q_scales[:, qcol : qcol + 128],
+                    rhs=k_codes[:, 512 * g : 512 * g + 512].bitcast(FP8X4),
+                    rhs_scale=k_scales[:, 512 * g : 512 * g + 512],
+                    start=(g == 0),
+                    stop=(g == 1 or lone),
+                )
+            accs[(i, t)] = acc
+
+        def add_up(i, t):
+            if t == 0:
+                results[i] = work.tile([P, 2, C], F32, tag="res", bufs=STORE_LAG + 2, name="res")
+            res = results[i]
+            x, low = shifted[i]
+            a_seg = accs[(i, t)][:].rearrange("p (tt s r) -> p s r tt", tt=4, s=4)
+            o_seg = res[:, t, :].rearrange("p (s r tt) -> p s r tt", s=4, tt=4)
+            x_seg = x[:].rearrange("p s (r tt) -> p s r tt", tt=4)
+            l_seg = low[:].rearrange("p s (r tt) -> p s r tt", tt=4)
+            if t == 0:
+                nc.vector.tensor_tensor(out=o_seg[:, 0:2], in0=a_seg[:, 0:2], in1=x_seg[:, 0:2], op=ADD)
+                nc.vector.tensor_tensor(out=o_seg[:, 2:4], in0=a_seg[:, 2:4], in1=l_seg[:, 2:4], op=ADD)
+            else:
+                nc.vector.tensor_tensor(out=o_seg[:, 1:3], in0=a_seg[:, 1:3], in1=x_seg[:, 2:4], op=ADD)
+                nc.vector.tensor_tensor(out=o_seg[:, 0:4:3], in0=a_seg[:, 0:4:3], in1=l_seg[:, 0:2], op=ADD)
+
+        stored = [0]
+
+        def store_up_to(last, queue):
+            while stored[0] <= last:
+                queue.dma_start(out=o_view[stored[0]], in_=results[stored[0]][:])
+                stored[0] += 1
+
+        for s in range(-Q_AHEAD, NBLK + 1):
+            j_t, j_b, j_w, j_r, i_a = s + Q_AHEAD, s + B_AHEAD, s + B_AHEAD - 1, s + B_AHEAD - 2, s - 1
+            has_k = 0 <= s < NBLK
+            has_a = 0 <= i_a
+            if s in EARLY_K_LOADS:
+                load_k(EARLY_K_LOADS[s])
+            elif 4 <= s + K_LOAD < NBLK:
+                load_k(s + K_LOAD)
+            if 2 <= s + Q_LOAD < NBLK:
+                load_pair_rows(s + Q_LOAD, q_view[s + Q_LOAD])
+            store_up_to(i_a - STORE_LAG if s + K_LOAD < NBLK else i_a - 1, nc.sync)
+            if 0 <= j_w < NBLK:
+                park_write(j_w)
+            if 0 <= j_r < NBLK:
+                read_back(j_r)
+            if 0 <= j_t - 1 < NBLK:
+                quantise_q(j_t - 1)
+            has_b = 0 <= j_b < NBLK
+            if has_k:
+                transpose_k(s, (0, 1, 2))
+            if has_a:
+                content(i_a, 0)
+            if has_b:
+                positions(j_b, 0)
+            if has_a:
+                add_up(i_a, 0)
+            if has_k:
+                transpose_k(s, (3,))
+            if j_t < NBLK:
+                transpose_pair_rows(j_t, True, (0, 0))
+            if s == -Q_AHEAD:
+                project()
+            if has_k:
+                quantise_k(s)
+            if has_a:
+                content(i_a, 1)
+            if has_b:
+                positions(j_b, 1)
+                park_rows(j_b)
+            if has_a:
+                add_up(i_a, 1)
+        store_up_to(NBLK - 1, nc.sync)

@@ -229,9 +229,7 @@ def tile_gemma3naudiorelativepositionembedding_pa_t_kernel(tc, queries, keys, si
             q_codes, q_scales = q_mx[i]
             k_codes, k_scales = k_mx[i]
             acc = psum.tile([P, C], F32, tag="ac", bufs=2)
-            for g in (-1, 0, 1):
-                lone = g < 0
-                g = max(g, 0)
+            for g in range(2):
                 qcol = 256 * g + 128 * t
                 nc.tensor.matmul_mx(
                     out=acc[:],
@@ -240,7 +238,7 @@ def tile_gemma3naudiorelativepositionembedding_pa_t_kernel(tc, queries, keys, si
                     rhs=k_codes[:, 512 * g : 512 * g + 512].bitcast(FP8X4),
                     rhs_scale=k_scales[:, 512 * g : 512 * g + 512],
                     start=(g == 0),
-                    stop=(g == 1 or lone),
+                    stop=(g == 1),
                 )
             accs[(i, t)] = acc
 

@@ -21,7 +21,9 @@ PITCH = 128 + 2 * F
 Q_AHEAD = 8
 B_AHEAD = 4
 K_LOAD = 2
-Q_LOAD = Q_AHEAD + 2
+Q_SORT = Q_AHEAD + 1
+Q_FIRST_SORTED = 2
+Q_LOAD = Q_AHEAD + 3
 STORE_LAG = 7
 EARLY_K_LOADS = {-6: 0, -5: 1, -3: 2, -1: 3}
 
@@ -46,6 +48,7 @@ def tile_gemma3naudiorelativepositionembedding_pa_t_kernel(tc, queries, keys, si
         ctx.enter_context(tc.manual_schedule())
 
         pair_raw = {}
+        pair_sorted = {}
         k_raw = {}
         pair_grouped = {}
         q_mx = {}
@@ -70,7 +73,7 @@ def tile_gemma3naudiorelativepositionembedding_pa_t_kernel(tc, queries, keys, si
         load_pair_rows("s", s_view)
         for h in range(4):
             load_pair_rows("w%d" % h, w_view[h // 2, h % 2])
-        for n in range(2):
+        for n in range(Q_LOAD - Q_AHEAD):
             load_pair_rows(n, q_view[n])
 
         ident = const.tile([P, P], F32, name="ident")
@@ -87,8 +90,17 @@ def tile_gemma3naudiorelativepositionembedding_pa_t_kernel(tc, queries, keys, si
             else:
                 nc.vector.tensor_copy(out=dst, in_=src)
 
+        def sort_pair_rows(key):
+            dst = work.tile([P, 2 * D], BF16, tag="qs", bufs=3)
+            nc.vector.tensor_copy(
+                out=dst[:].bitcast(F32).rearrange("p (q u m) -> p q u m", u=2, m=128),
+                in_=pair_raw[key][:].bitcast(F32).rearrange("p (q m u) -> p q u m", u=2, m=128),
+            )
+            pair_sorted[key] = dst
+
         def transpose_pair_rows(key, natural, engines):
-            words = pair_raw[key][:].bitcast(F32)
+            ordered = key in pair_sorted
+            words = (pair_sorted[key] if ordered else pair_raw[key])[:].bitcast(F32)
             grouped = work.tile([P, 2 * U * 4], BF16, tag="qg", bufs=3, align_bytes=64)
             g32 = grouped[:].bitcast(F32).rearrange("p (g c u) -> p g c u", g=2, u=2)
             for g in range(2):
@@ -96,7 +108,11 @@ def tile_gemma3naudiorelativepositionembedding_pa_t_kernel(tc, queries, keys, si
                 for e in range(2):
                     for u2 in range(2):
                         col = 512 * e + 256 * g
-                        nc.tensor.transpose(bank[:, 2 * e + u2, :], words[:, col + u2 : col + 256 : 2], ident[:])
+                        if ordered:
+                            src = words[:, col + 128 * u2 : col + 128 * u2 + 128]
+                        else:
+                            src = words[:, col + u2 : col + 256 : 2]
+                        nc.tensor.transpose(bank[:, 2 * e + u2, :], src, ident[:])
                 if natural:
                     dst = g32[:, g].rearrange("p (r e) u -> p r e u", e=2)
                     bsrc = bank[:].rearrange("p (e u) r -> p r e u", e=2)
@@ -214,7 +230,7 @@ def tile_gemma3naudiorelativepositionembedding_pa_t_kernel(tc, queries, keys, si
                     col = 512 * tt + 256 * (w // 2)
                     nc.tensor.transpose(bank[:, w, :], words[:, col + w % 2 : col + 256 : 2], ident[:])
                 copy_out(
-                    1 if tt == 3 else 0,
+                    0,
                     g32[:, :, 128 * tt : 128 * tt + 128, :],
                     bank[:].rearrange("p (g u) r -> p g r u", g=2),
                 )
@@ -273,7 +289,7 @@ def tile_gemma3naudiorelativepositionembedding_pa_t_kernel(tc, queries, keys, si
                 load_k(EARLY_K_LOADS[s])
             elif 4 <= s + K_LOAD < NBLK:
                 load_k(s + K_LOAD)
-            if 2 <= s + Q_LOAD < NBLK:
+            if Q_LOAD - Q_AHEAD <= s + Q_LOAD < NBLK:
                 load_pair_rows(s + Q_LOAD, q_view[s + Q_LOAD])
             store_up_to(i_a - STORE_LAG if s + K_LOAD < NBLK else i_a - 1, nc.sync)
             if 0 <= j_w < NBLK:
@@ -282,6 +298,8 @@ def tile_gemma3naudiorelativepositionembedding_pa_t_kernel(tc, queries, keys, si
                 read_back(j_r)
             if 0 <= j_t - 1 < NBLK:
                 quantise_q(j_t - 1)
+            if Q_FIRST_SORTED <= s + Q_SORT < NBLK:
+                sort_pair_rows(s + Q_SORT)
             has_b = 0 <= j_b < NBLK
             if has_k:
                 transpose_k(s, (0, 1, 2))

@@ -17,14 +17,23 @@ U = 256
 C = 512
 D = 1024
 F = 256
-PITCH = 128 + 2 * F
-Q_AHEAD = 8
-B_AHEAD = 4
+PARKED = 2
+RING = 2 * F * PARKED
+PITCH = 128 + RING
+Q_AHEAD = 7
+B_AHEAD = 5
+WRITE_LAG = 1
+READ_LAG = 3
+MASK_LAG = 5
+X_BUFS = 3
 K_LOAD = 2
-Q_SORT = Q_AHEAD + 1
-Q_FIRST_SORTED = 2
+SORT_LEAD = 1
+Q_SORT_FROM = 4
+W_SORT_FROM = 9
+K_SORT_FROM = 4
+K_ON_VECTOR = ()
 Q_LOAD = Q_AHEAD + 3
-STORE_LAG = 7
+STORE_LAG = 5
 EARLY_K_LOADS = {-6: 0, -5: 1, -3: 2, -1: 3}
 
 FLOPS = 2 * F * D * D + NBLK * 2 * U * D * (C + F)
@@ -37,7 +46,7 @@ def tile_gemma3naudiorelativepositionembedding_pa_t_kernel(tc, queries, keys, si
     s_view = sin_emb.rearrange("(p e) i -> p (e i)", e=2)
     w_view = pos_w.rearrange("(g p t e) i -> g t p (e i)", g=2, t=2, e=2)
     o_view = out.rearrange("b h w (t p) c -> (b h w) p t c", t=2)
-    o_flat = out.rearrange("b h w u c -> (b h w) (u c)")
+    o_flat = out.rearrange("(b e) h w u c -> (b e h w u c)", e=1)
 
     with ExitStack() as ctx:
         const = ctx.enter_context(tc.tile_pool(name="const", bufs=1))
@@ -50,6 +59,7 @@ def tile_gemma3naudiorelativepositionembedding_pa_t_kernel(tc, queries, keys, si
         pair_raw = {}
         pair_sorted = {}
         k_raw = {}
+        k_sorted = {}
         pair_grouped = {}
         q_mx = {}
         k_grouped = {}
@@ -79,8 +89,8 @@ def tile_gemma3naudiorelativepositionembedding_pa_t_kernel(tc, queries, keys, si
         ident = const.tile([P, P], F32, name="ident")
         make_identity(nc, ident[:])
         lows = []
-        for n in range(B_AHEAD + 2):
-            low = const.tile([P, 4, 128], F32, name="low%d" % n)
+        for n in range(X_BUFS):
+            low = const.tile([P, PARKED, 4, 128], F32, name="low%d" % n)
             nc.gpsimd.memset(low[:], 0.0)
             lows.append(low)
 
@@ -90,13 +100,21 @@ def tile_gemma3naudiorelativepositionembedding_pa_t_kernel(tc, queries, keys, si
             else:
                 nc.vector.tensor_copy(out=dst, in_=src)
 
-        def sort_pair_rows(key):
-            dst = work.tile([P, 2 * D], BF16, tag="qs", bufs=3)
-            nc.vector.tensor_copy(
-                out=dst[:].bitcast(F32).rearrange("p (q u m) -> p q u m", u=2, m=128),
-                in_=pair_raw[key][:].bitcast(F32).rearrange("p (q m u) -> p q u m", u=2, m=128),
+        def sort_words(engine, dst, src, dtype):
+            engine.tensor_copy(
+                out=dst.bitcast(dtype).rearrange("p (q u m) -> p q u m", u=2, m=128),
+                in_=src.bitcast(dtype).rearrange("p (q m u) -> p q u m", u=2, m=128),
             )
+
+        def sort_pair_rows(key, engine, dtype):
+            dst = work.tile([P, 2 * D], BF16, tag="qs", bufs=3)
+            sort_words(engine, dst[:], pair_raw[key][:], dtype)
             pair_sorted[key] = dst
+
+        def sort_k(i, engine, dtype):
+            dst = work.tile([P, (4 - K_SORT_FROM) * D], BF16, tag="ks")
+            sort_words(engine, dst[:], k_raw[i][:, K_SORT_FROM * D :], dtype)
+            k_sorted[i] = dst
 
         def transpose_pair_rows(key, natural, engines):
             ordered = key in pair_sorted
@@ -189,34 +207,42 @@ def tile_gemma3naudiorelativepositionembedding_pa_t_kernel(tc, queries, keys, si
 
         def park_rows(j):
             bd = bds[j]
-            park = work.tile([P, PITCH], F32, tag="park", bufs=3)
-            nc.scalar.copy(out=park[:, 128:PITCH], in_=bd[:].rearrange("p t f -> p (t f)"))
-            nc.scalar.copy(out=park[:, 0:128], in_=bd[:, 1, 128:256])
-            parks[j] = park
+            b = j % PARKED
+            if b == 0:
+                parks[j // PARKED] = work.tile([P, PITCH], F32, tag="park", bufs=3, name="park")
+            park = parks[j // PARKED]
+            nc.scalar.copy(out=park[:, 128 + 512 * b : 640 + 512 * b], in_=bd[:].rearrange("p t f -> p (t f)"))
+            if b == PARKED - 1:
+                nc.scalar.copy(out=park[:, 0:128], in_=bd[:, 1, 128:256])
 
-        def park_write(j):
+        def park_write(n):
+            base = n * PARKED * U * C
             nc.sync.dma_start(
-                out=o_flat[j, 0 : P * PITCH].rearrange("(p s) -> p s", s=PITCH), in_=parks[j][:]
+                out=o_flat[base : base + P * PITCH].rearrange("(p s) -> p s", s=PITCH), in_=parks[n][:]
             )
 
-        def read_back(j):
-            x = keep.tile([P, 4, 128], F32, tag="x", bufs=B_AHEAD + 2)
+        def read_back(n):
+            base = n * PARKED * U * C + 128
+            x = keep.tile([P, 4 * PARKED, 128], F32, tag="x", bufs=X_BUFS)
             nc.sync.dma_start(
                 out=x[:].rearrange("p s j -> p (s j)"),
-                in_=o_flat[j, 128 : 128 + P * (PITCH - 1)].rearrange("(p s) -> p s", s=PITCH - 1)[:, 0:512],
+                in_=o_flat[base : base + P * (PITCH - 1)].rearrange("(p s) -> p s", s=PITCH - 1)[:, 0:RING],
             )
-            low = lows[j % (B_AHEAD + 2)]
-            for n in range(2):
-                shared = x[:, 2 * n, :]
+            shifted[n] = x
+
+        def mask(n):
+            x, low = shifted[n], lows[n % X_BUFS]
+            for tile in range(2 * PARKED):
+                before = (tile - 1) % (2 * PARKED)
+                shared = x[:, 2 * tile, :]
                 nc.gpsimd.affine_select(
-                    out=low[:, 1 + n, :], in_=shared, pattern=[[-1, 128]],
+                    out=low[:, before // 2, 2 - before % 2, :], in_=shared, pattern=[[-1, 128]],
                     compare_op=IS_GE, fill=0.0, base=-1, channel_multiplier=1,
                 )
                 nc.gpsimd.affine_select(
                     out=shared, in_=shared, pattern=[[1, 128]],
                     compare_op=IS_GE, fill=0.0, base=0, channel_multiplier=-1,
                 )
-            shifted[j] = (x, low)
 
         def transpose_k(i, banks):
             words = k_raw[i][:].bitcast(F32)
@@ -227,10 +253,15 @@ def tile_gemma3naudiorelativepositionembedding_pa_t_kernel(tc, queries, keys, si
             for tt in banks:
                 bank = psum.tile([P, 4, P], F32, tag="tp", bufs=4)
                 for w in range(4):
-                    col = 512 * tt + 256 * (w // 2)
-                    nc.tensor.transpose(bank[:, w, :], words[:, col + w % 2 : col + 256 : 2], ident[:])
+                    if tt >= K_SORT_FROM:
+                        col = 512 * (tt - K_SORT_FROM) + 128 * w
+                        src = k_sorted[i][:].bitcast(F32)[:, col : col + 128]
+                    else:
+                        col = 512 * tt + 256 * (w // 2)
+                        src = words[:, col + w % 2 : col + 256 : 2]
+                    nc.tensor.transpose(bank[:, w, :], src, ident[:])
                 copy_out(
-                    0,
+                    1 if tt in K_ON_VECTOR else 0,
                     g32[:, :, 128 * tt : 128 * tt + 128, :],
                     bank[:].rearrange("p (g u) r -> p g r u", g=2),
                 )
@@ -244,7 +275,7 @@ def tile_gemma3naudiorelativepositionembedding_pa_t_kernel(tc, queries, keys, si
         def content(i, t):
             q_codes, q_scales = q_mx[i]
             k_codes, k_scales = k_mx[i]
-            acc = psum.tile([P, C], F32, tag="ac", bufs=2)
+            acc = psum.tile([P, C], F32, tag="bd" if i == NBLK - 1 else "ac", bufs=2, name="acc")
             for g in range(2):
                 qcol = 256 * g + 128 * t
                 nc.tensor.matmul_mx(
@@ -262,11 +293,12 @@ def tile_gemma3naudiorelativepositionembedding_pa_t_kernel(tc, queries, keys, si
             if t == 0:
                 results[i] = work.tile([P, 2, C], F32, tag="res", bufs=STORE_LAG + 2, name="res")
             res = results[i]
-            x, low = shifted[i]
+            n, b = divmod(i, PARKED)
+            x, low = shifted[n][:, 4 * b : 4 * b + 4, :], lows[n % X_BUFS][:, b]
             a_seg = accs[(i, t)][:].rearrange("p (tt s r) -> p s r tt", tt=4, s=4)
             o_seg = res[:, t, :].rearrange("p (s r tt) -> p s r tt", s=4, tt=4)
-            x_seg = x[:].rearrange("p s (r tt) -> p s r tt", tt=4)
-            l_seg = low[:].rearrange("p s (r tt) -> p s r tt", tt=4)
+            x_seg = x.rearrange("p s (r tt) -> p s r tt", tt=4)
+            l_seg = low.rearrange("p s (r tt) -> p s r tt", tt=4)
             if t == 0:
                 nc.vector.tensor_tensor(out=o_seg[:, 0:2], in0=a_seg[:, 0:2], in1=x_seg[:, 0:2], op=ADD)
                 nc.vector.tensor_tensor(out=o_seg[:, 2:4], in0=a_seg[:, 2:4], in1=l_seg[:, 2:4], op=ADD)
@@ -281,10 +313,15 @@ def tile_gemma3naudiorelativepositionembedding_pa_t_kernel(tc, queries, keys, si
                 queue.dma_start(out=o_view[stored[0]], in_=results[stored[0]][:])
                 stored[0] += 1
 
-        for s in range(-Q_AHEAD, NBLK + 1):
-            j_t, j_b, j_w, j_r, i_a = s + Q_AHEAD, s + B_AHEAD, s + B_AHEAD - 1, s + B_AHEAD - 2, s - 1
+        for s in range(-Q_AHEAD, NBLK + 2):
+            j_t, j_b, i_c, i_a = s + Q_AHEAD, s + B_AHEAD, s - 1, s - 2
             has_k = 0 <= s < NBLK
-            has_a = 0 <= i_a
+            has_b = 0 <= j_b < NBLK
+
+            def pair_due(lag):
+                j = s + B_AHEAD - lag
+                return j // PARKED if PARKED - 1 <= j < NBLK and j % PARKED == PARKED - 1 else None
+
             if s in EARLY_K_LOADS:
                 load_k(EARLY_K_LOADS[s])
             elif 4 <= s + K_LOAD < NBLK:
@@ -292,36 +329,34 @@ def tile_gemma3naudiorelativepositionembedding_pa_t_kernel(tc, queries, keys, si
             if Q_LOAD - Q_AHEAD <= s + Q_LOAD < NBLK:
                 load_pair_rows(s + Q_LOAD, q_view[s + Q_LOAD])
             store_up_to(i_a - STORE_LAG if s + K_LOAD < NBLK else i_a - 1, nc.sync)
-            if 0 <= j_w < NBLK:
-                park_write(j_w)
-            if 0 <= j_r < NBLK:
-                read_back(j_r)
+            if pair_due(WRITE_LAG) is not None:
+                park_write(pair_due(WRITE_LAG))
+            if pair_due(READ_LAG) is not None:
+                read_back(pair_due(READ_LAG))
+            if pair_due(MASK_LAG) is not None:
+                mask(pair_due(MASK_LAG))
             if 0 <= j_t - 1 < NBLK:
                 quantise_q(j_t - 1)
-            if Q_FIRST_SORTED <= s + Q_SORT < NBLK:
-                sort_pair_rows(s + Q_SORT)
-            has_b = 0 <= j_b < NBLK
-            if has_k:
-                transpose_k(s, (0, 1, 2))
-            if has_a:
-                content(i_a, 0)
-            if has_b:
-                positions(j_b, 0)
-            if has_a:
+            if 0 <= i_a:
                 add_up(i_a, 0)
+                add_up(i_a, 1)
+            if Q_SORT_FROM <= j_t + SORT_LEAD < NBLK:
+                sort_pair_rows(j_t + SORT_LEAD, nc.vector, F32)
+            if K_SORT_FROM < 4 and 0 <= s + SORT_LEAD < NBLK:
+                sort_k(s + SORT_LEAD, nc.vector, F32)
             if has_k:
-                transpose_k(s, (3,))
+                transpose_k(s, (0, 1, 2, 3))
             if j_t < NBLK:
-                transpose_pair_rows(j_t, True, (0, 0))
+                transpose_pair_rows(j_t, True, (0, 0) if has_k else (0, 1))
             if s == -Q_AHEAD:
                 project()
             if has_k:
                 quantise_k(s)
-            if has_a:
-                content(i_a, 1)
             if has_b:
+                positions(j_b, 0)
                 positions(j_b, 1)
                 park_rows(j_b)
-            if has_a:
-                add_up(i_a, 1)
+            if 0 <= i_c < NBLK:
+                content(i_c, 0)
+                content(i_c, 1)
         store_up_to(NBLK - 1, nc.sync)

@@ -26,6 +26,7 @@ WRITE_LAG = 1
 READ_LAG = 3
 MASK_LAG = 5
 X_BUFS = 3
+PARK_BUFS = 3
 K_LOAD = 2
 SORT_LEAD = 1
 Q_SORT_FROM = 4
@@ -209,7 +210,7 @@ def tile_gemma3naudiorelativepositionembedding_pa_t_kernel(tc, queries, keys, si
             bd = bds[j]
             b = j % PARKED
             if b == 0:
-                parks[j // PARKED] = work.tile([P, PITCH], F32, tag="park", bufs=3, name="park")
+                parks[j // PARKED] = work.tile([P, PITCH], F32, tag="park", bufs=PARK_BUFS, name="park")
             park = parks[j // PARKED]
             nc.scalar.copy(out=park[:, 128 + 512 * b : 640 + 512 * b], in_=bd[:].rearrange("p t f -> p (t f)"))
             if b == PARKED - 1:
@@ -345,18 +346,21 @@ def tile_gemma3naudiorelativepositionembedding_pa_t_kernel(tc, queries, keys, si
             if K_SORT_FROM < 4 and 0 <= s + SORT_LEAD < NBLK:
                 sort_k(s + SORT_LEAD, nc.vector, F32)
             if has_k:
-                transpose_k(s, (0, 1, 2, 3))
+                transpose_k(s, (0, 1))
+            if has_b:
+                positions(j_b, 0)
+                positions(j_b, 1)
+                park_rows(j_b)
+            if has_k:
+                transpose_k(s, (2, 3))
+            if 0 <= i_c < NBLK:
+                content(i_c, 0)
             if j_t < NBLK:
                 transpose_pair_rows(j_t, True, (0, 0) if has_k else (0, 1))
             if s == -Q_AHEAD:
                 project()
             if has_k:
                 quantise_k(s)
-            if has_b:
-                positions(j_b, 0)
-                positions(j_b, 1)
-                park_rows(j_b)
             if 0 <= i_c < NBLK:
-                content(i_c, 0)
                 content(i_c, 1)
         store_up_to(NBLK - 1, nc.sync)

@@ -29,9 +29,9 @@ X_BUFS = 3
 PARK_BUFS = 3
 K_LOAD = 2
 SORT_LEAD = 1
-Q_SORT_FROM = 4
+Q_SORT_FROM = 6
 W_SORT_FROM = 9
-K_SORT_FROM = 4
+K_SORT_FROM = 3
 K_ON_VECTOR = ()
 Q_LOAD = Q_AHEAD + 3
 STORE_LAG = 5

@@ -17,19 +17,19 @@ U = 256
 C = 512
 D = 1024
 F = 256
-PARKED = 2
+PARKED = 4
 RING = 2 * F * PARKED
 PITCH = 128 + RING
-Q_AHEAD = 7
-B_AHEAD = 5
+Q_AHEAD = 9
+B_AHEAD = 7
 WRITE_LAG = 1
-READ_LAG = 3
-MASK_LAG = 5
-X_BUFS = 3
-PARK_BUFS = 3
+READ_LAG = 4
+MASK_LAG = 6
+X_BUFS = 2
+PARK_BUFS = 2
 K_LOAD = 2
 SORT_LEAD = 1
-Q_SORT_FROM = 6
+Q_SORT_FROM = 5
 W_SORT_FROM = 9
 K_SORT_FROM = 3
 K_ON_VECTOR = ()
@@ -91,8 +91,7 @@ def tile_gemma3naudiorelativepositionembedding_pa_t_kernel(tc, queries, keys, si
         make_identity(nc, ident[:])
         lows = []
         for n in range(X_BUFS):
-            low = const.tile([P, PARKED, 4, 128], F32, name="low%d" % n)
-            nc.gpsimd.memset(low[:], 0.0)
+            low = const.tile([P, 2 * PARKED, 128], F32, name="low%d" % n)
             lows.append(low)
 
         def copy_out(engine, dst, src):
@@ -146,9 +145,9 @@ def tile_gemma3naudiorelativepositionembedding_pa_t_kernel(tc, queries, keys, si
 
         s_codes = const.tile([P, 2 * F], U32, name="s_codes", align_bytes=64)
         s_scales = const.tile([P, 2 * F], U8, name="s_scales", align_bytes=64)
-        w_codes = const.tile([P, 4, 512], U32, name="w_codes", align_bytes=64)
+        w_codes = work.tile([P, 4, 512], U32, tag="kg", align_bytes=64, name="w_codes")
         w_scales = const.tile([P, 4, 512], U8, name="w_scales", align_bytes=64)
-        p_grouped = const.tile([P, 2 * F * 4], BF16, name="p_grouped", align_bytes=64)
+        p_grouped = work.tile([P, 2 * F * 4], BF16, tag="kg", align_bytes=64, name="p_grouped")
         pg = p_grouped[:].rearrange("p (g f t) -> p g f t", g=2, t=4)
         p_codes = const.tile([P, 2 * F], U32, name="p_codes", align_bytes=64)
         p_scales = const.tile([P, 2 * F], U8, name="p_scales", align_bytes=64)
@@ -237,7 +236,7 @@ def tile_gemma3naudiorelativepositionembedding_pa_t_kernel(tc, queries, keys, si
                 before = (tile - 1) % (2 * PARKED)
                 shared = x[:, 2 * tile, :]
                 nc.gpsimd.affine_select(
-                    out=low[:, before // 2, 2 - before % 2, :], in_=shared, pattern=[[-1, 128]],
+                    out=low[:, before, :], in_=shared, pattern=[[-1, 128]],
                     compare_op=IS_GE, fill=0.0, base=-1, channel_multiplier=1,
                 )
                 nc.gpsimd.affine_select(
@@ -290,22 +289,26 @@ def tile_gemma3naudiorelativepositionembedding_pa_t_kernel(tc, queries, keys, si
                 )
             accs[(i, t)] = acc
 
+        def segments(i, t):
+            return (
+                accs[(i, t)][:].rearrange("p (tt s r) -> p s r tt", tt=4, s=4),
+                results[i][:, t, :].rearrange("p (s r tt) -> p s r tt", s=4, tt=4),
+            )
+
+        def copy_rest(i, t):
+            if t == 0:
+                results[i] = work.tile([P, 2, C], F32, tag="res", bufs=STORE_LAG + 3, name="res")
+            a_seg, o_seg = segments(i, t)
+            rest = 3 - 3 * t
+            nc.scalar.copy(out=o_seg[:, rest : rest + 1], in_=a_seg[:, rest : rest + 1])
+
         def add_up(i, t):
-            if t == 0:
-                results[i] = work.tile([P, 2, C], F32, tag="res", bufs=STORE_LAG + 2, name="res")
-            res = results[i]
             n, b = divmod(i, PARKED)
-            x, low = shifted[n][:, 4 * b : 4 * b + 4, :], lows[n % X_BUFS][:, b]
-            a_seg = accs[(i, t)][:].rearrange("p (tt s r) -> p s r tt", tt=4, s=4)
-            o_seg = res[:, t, :].rearrange("p (s r tt) -> p s r tt", s=4, tt=4)
-            x_seg = x.rearrange("p s (r tt) -> p s r tt", tt=4)
-            l_seg = low.rearrange("p s (r tt) -> p s r tt", tt=4)
-            if t == 0:
-                nc.vector.tensor_tensor(out=o_seg[:, 0:2], in0=a_seg[:, 0:2], in1=x_seg[:, 0:2], op=ADD)
-                nc.vector.tensor_tensor(out=o_seg[:, 2:4], in0=a_seg[:, 2:4], in1=l_seg[:, 2:4], op=ADD)
-            else:
-                nc.vector.tensor_tensor(out=o_seg[:, 1:3], in0=a_seg[:, 1:3], in1=x_seg[:, 2:4], op=ADD)
-                nc.vector.tensor_tensor(out=o_seg[:, 0:4:3], in0=a_seg[:, 0:4:3], in1=l_seg[:, 0:2], op=ADD)
+            x_seg = shifted[n][:, 4 * b + 2 * t : 4 * b + 2 * t + 2, :].rearrange("p s (r tt) -> p s r tt", tt=4)
+            l_seg = lows[n % X_BUFS][:, 2 * b + t : 2 * b + t + 1, :].rearrange("p s (r tt) -> p s r tt", tt=4)
+            a_seg, o_seg = segments(i, t)
+            nc.vector.tensor_tensor(out=o_seg[:, t : t + 2], in0=a_seg[:, t : t + 2], in1=x_seg, op=ADD)
+            nc.vector.tensor_tensor(out=o_seg[:, t + 2 : t + 3], in0=a_seg[:, t + 2 : t + 3], in1=l_seg, op=ADD)
 
         stored = [0]
 
@@ -347,7 +350,7 @@ def tile_gemma3naudiorelativepositionembedding_pa_t_kernel(tc, queries, keys, si
                 sort_k(s + SORT_LEAD, nc.vector, F32)
             if has_k:
                 transpose_k(s, (0, 1))
-            if has_b:
+            if has_b and has_k:
                 positions(j_b, 0)
                 positions(j_b, 1)
                 park_rows(j_b)
@@ -361,6 +364,12 @@ def tile_gemma3naudiorelativepositionembedding_pa_t_kernel(tc, queries, keys, si
                 project()
             if has_k:
                 quantise_k(s)
+            if has_b and not has_k:
+                positions(j_b, 0)
+                positions(j_b, 1)
+                park_rows(j_b)
             if 0 <= i_c < NBLK:
                 content(i_c, 1)
+                copy_rest(i_c, 0)
+                copy_rest(i_c, 1)
         store_up_to(NBLK - 1, nc.sync)

@@ -356,8 +356,6 @@ def tile_gemma3naudiorelativepositionembedding_pa_t_kernel(tc, queries, keys, si
                 park_rows(j_b)
             if has_k:
                 transpose_k(s, (2, 3))
-            if 0 <= i_c < NBLK:
-                content(i_c, 0)
             if j_t < NBLK:
                 transpose_pair_rows(j_t, True, (0, 0) if has_k else (0, 1))
             if s == -Q_AHEAD:
@@ -369,6 +367,7 @@ def tile_gemma3naudiorelativepositionembedding_pa_t_kernel(tc, queries, keys, si
                 positions(j_b, 1)
                 park_rows(j_b)
             if 0 <= i_c < NBLK:
+                content(i_c, 0)
                 content(i_c, 1)
                 copy_rest(i_c, 0)
                 copy_rest(i_c, 1)

@@ -21,20 +21,20 @@ PARKED = 4
 RING = 2 * F * PARKED
 PITCH = 128 + RING
 Q_AHEAD = 9
-B_AHEAD = 7
+B_AHEAD = 6
 WRITE_LAG = 1
-READ_LAG = 4
-MASK_LAG = 6
+READ_LAG = 2
+MASK_LAG = 4
 X_BUFS = 2
 PARK_BUFS = 2
 K_LOAD = 2
 SORT_LEAD = 1
-Q_SORT_FROM = 5
+Q_SORT_FROM = 9
 W_SORT_FROM = 9
 K_SORT_FROM = 3
 K_ON_VECTOR = ()
 Q_LOAD = Q_AHEAD + 3
-STORE_LAG = 5
+STORE_LAG = 4
 EARLY_K_LOADS = {-6: 0, -5: 1, -3: 2, -1: 3}
 
 FLOPS = 2 * F * D * D + NBLK * 2 * U * D * (C + F)
@@ -42,10 +42,10 @@ FLOPS = 2 * F * D * D + NBLK * 2 * U * D * (C + F)
 
 def tile_gemma3naudiorelativepositionembedding_pa_t_kernel(tc, queries, keys, sin_emb, pos_w, out):
     nc = tc.nc
-    q_view = queries.rearrange("b w (p e) h d -> (b w) p (e h d)", e=2)
+    q_view = queries.rearrange("b (n w) u h d -> (b n) (w u) (h d)", w=2).rearrange("n (p e) d -> n p (e d)", e=4)
     k_view = keys.rearrange("b w (p t) h d -> (b w) p (t h d)", t=4)
     s_view = sin_emb.rearrange("(p e) i -> p (e i)", e=2)
-    w_view = pos_w.rearrange("(g p t e) i -> g t p (e i)", g=2, t=2, e=2)
+    w_view = pos_w.rearrange("(g p t) i -> g p (t i)", g=2, t=4)
     o_view = out.rearrange("b h w (t p) c -> (b h w) p t c", t=2)
     o_flat = out.rearrange("(b e) h w u c -> (b e h w u c)", e=1)
 
@@ -53,12 +53,15 @@ def tile_gemma3naudiorelativepositionembedding_pa_t_kernel(tc, queries, keys, si
         const = ctx.enter_context(tc.tile_pool(name="const", bufs=1))
         raws = ctx.enter_context(tc.tile_pool(name="raws", bufs=6))
         work = ctx.enter_context(tc.tile_pool(name="work", bufs=2))
-        keep = ctx.enter_context(tc.tile_pool(name="keep", bufs=Q_AHEAD + 3))
+        keep = ctx.enter_context(tc.tile_pool(name="keep", bufs=Q_AHEAD // 2 + 2))
         psum = ctx.enter_context(tc.psum_pool(name="psum", bufs=2))
         ctx.enter_context(tc.manual_schedule())
 
         pair_raw = {}
         pair_sorted = {}
+        q_raw = {}
+        q_sorted = {}
+        q_grouped = {}
         k_raw = {}
         k_sorted = {}
         pair_grouped = {}
@@ -72,20 +75,28 @@ def tile_gemma3naudiorelativepositionembedding_pa_t_kernel(tc, queries, keys, si
         results = {}
 
         def load_pair_rows(key, src):
-            raw = raws.tile([P, 2 * D], BF16, tag="qraw", bufs=8)
-            nc.sync.dma_start(out=raw[:], in_=src)
-            pair_raw[key] = raw
+            raw = raws.tile([P, 4 * D], BF16, tag="q4raw", bufs=4)
+            nc.sync.dma_start(out=raw[:, 0 : 2 * D], in_=src)
+            pair_raw[key] = raw[:, 0 : 2 * D]
 
         def load_k(i):
             raw = raws.tile([P, 4 * D], BF16, tag="kraw", bufs=4)
             nc.sync.dma_start(out=raw[:], in_=k_view[i])
             k_raw[i] = raw
 
+        def load_q(n):
+            raw = raws.tile([P, 4 * D], BF16, tag="q4raw", bufs=4)
+            nc.sync.dma_start(out=raw[:], in_=q_view[n])
+            q_raw[n] = raw
+
         load_pair_rows("s", s_view)
-        for h in range(4):
-            load_pair_rows("w%d" % h, w_view[h // 2, h % 2])
-        for n in range(Q_LOAD - Q_AHEAD):
-            load_pair_rows(n, q_view[n])
+        for g in range(2):
+            raw = raws.tile([P, 4 * D], BF16, tag="q4raw", bufs=4, name="w_raw")
+            nc.sync.dma_start(out=raw[:], in_=w_view[g])
+            for h in range(2):
+                pair_raw["w%d" % (2 * g + h)] = raw[:, 2 * D * h : 2 * D * h + 2 * D]
+        for n in range(2):
+            load_q(n)
 
         ident = const.tile([P, P], F32, name="ident")
         make_identity(nc, ident[:])
@@ -108,8 +119,8 @@ def tile_gemma3naudiorelativepositionembedding_pa_t_kernel(tc, queries, keys, si
 
         def sort_pair_rows(key, engine, dtype):
             dst = work.tile([P, 2 * D], BF16, tag="qs", bufs=3)
-            sort_words(engine, dst[:], pair_raw[key][:], dtype)
-            pair_sorted[key] = dst
+            sort_words(engine, dst[:], pair_raw[key], dtype)
+            pair_sorted[key] = dst[:]
 
         def sort_k(i, engine, dtype):
             dst = work.tile([P, (4 - K_SORT_FROM) * D], BF16, tag="ks")
@@ -118,7 +129,7 @@ def tile_gemma3naudiorelativepositionembedding_pa_t_kernel(tc, queries, keys, si
 
         def transpose_pair_rows(key, natural, engines):
             ordered = key in pair_sorted
-            words = (pair_sorted[key] if ordered else pair_raw[key])[:].bitcast(F32)
+            words = (pair_sorted[key] if ordered else pair_raw[key]).bitcast(F32)
             grouped = work.tile([P, 2 * U * 4], BF16, tag="qg", bufs=3, align_bytes=64)
             g32 = grouped[:].bitcast(F32).rearrange("p (g c u) -> p g c u", g=2, u=2)
             for g in range(2):
@@ -139,6 +150,30 @@ def tile_gemma3naudiorelativepositionembedding_pa_t_kernel(tc, queries, keys, si
                     bsrc = bank[:].rearrange("p (e u) r -> p e r u", e=2)
                 copy_out(engines[g], dst, bsrc)
             pair_grouped[key] = grouped
+
+        def sort_q(n, g, engine, dtype):
+            dst = work.tile([P, 2 * D], BF16, tag="qs", bufs=3)
+            src = q_raw[n][:].bitcast(dtype).rearrange("p (e g m u) -> p g e u m", e=4, g=2, u=2)[:, g]
+            engine.tensor_copy(out=dst[:].bitcast(dtype).rearrange("p (e u m) -> p e u m", e=4, u=2), in_=src)
+            q_sorted[(n, g)] = dst
+
+        def transpose_q(n, g, engines):
+            grouped = work.tile([P, 2 * U * 4], BF16, tag="qg", bufs=3, align_bytes=64)
+            g32 = grouped[:].bitcast(F32).rearrange("p (b r e u) -> p b r e u", b=2, e=4, u=2)
+            ordered = (n, g) in q_sorted
+            for eh in range(2):
+                bank = psum.tile([P, 4, P], F32, tag="tp", bufs=4)
+                for k in range(4):
+                    e, u2 = 2 * eh + k // 2, k % 2
+                    if ordered:
+                        src = q_sorted[(n, g)][:].bitcast(F32)[:, 256 * e + 128 * u2 : 256 * e + 128 * u2 + 128]
+                    else:
+                        col = 512 * e + 256 * g
+                        src = q_raw[n][:].bitcast(F32)[:, col + u2 : col + 256 : 2]
+                    nc.tensor.transpose(bank[:, k, :], src, ident[:])
+                for_b = bank[:].rearrange("p (e u) (b r) -> p b r e u", e=2, b=2)
+                copy_out(engines[eh], g32[:, :, :, 2 * eh : 2 * eh + 2, :], for_b)
+            q_grouped[(n, g)] = grouped
 
         def quantise_pair_rows(key, codes, scales):
             nc.vector.quantize_mx(out=codes.bitcast(FP8X4), scales=scales, in_=pair_grouped[key][:])
@@ -182,23 +217,25 @@ def tile_gemma3naudiorelativepositionembedding_pa_t_kernel(tc, queries, keys, si
                     copy_out(fh, pg[:, g, 128 * fh : 128 * fh + 128, :], pb[:].rearrange("p t f -> p f t"))
             nc.vector.quantize_mx(out=p_codes[:].bitcast(FP8X4), scales=p_scales[:], in_=p_grouped[:])
 
-        def quantise_q(j):
-            q_codes = keep.tile([P, 2 * U], U32, tag="q_codes", align_bytes=64)
-            q_scales = keep.tile([P, 2 * U], U8, tag="q_scales", align_bytes=64)
-            quantise_pair_rows(j, q_codes[:], q_scales[:])
-            q_mx[j] = (q_codes, q_scales)
+        def quantise_q(n, g):
+            if g == 0:
+                q_codes = keep.tile([P, 2, 2 * U], U32, tag="q_codes", align_bytes=64)
+                q_scales = keep.tile([P, 2, 2 * U], U8, tag="q_scales", align_bytes=64)
+                q_mx[n] = (q_codes, q_scales)
+            q_codes, q_scales = q_mx[n]
+            nc.vector.quantize_mx(out=q_codes[:, g, :].bitcast(FP8X4), scales=q_scales[:, g, :], in_=q_grouped[(n, g)][:])
 
         def positions(j, t):
-            q_codes, q_scales = q_mx[j]
+            q_codes, q_scales = q_mx[j // 2]
             if t == 0:
                 bds[j] = psum.tile([P, 2, F], F32, tag="bd", bufs=2, name="bd")
             bd = bds[j]
             for g in range(2):
-                qcol = 256 * g + 128 * t
+                qcol = 256 * (j % 2) + 128 * t
                 nc.tensor.matmul_mx(
                     out=bd[:, t, :],
-                    lhsT=q_codes[:, qcol : qcol + 128].bitcast(FP8X4),
-                    lhsT_scale=q_scales[:, qcol : qcol + 128],
+                    lhsT=q_codes[:, g, qcol : qcol + 128].bitcast(FP8X4),
+                    lhsT_scale=q_scales[:, g, qcol : qcol + 128],
                     rhs=p_codes[:, 256 * g : 256 * g + 256].bitcast(FP8X4),
                     rhs_scale=p_scales[:, 256 * g : 256 * g + 256],
                     start=(g == 0),
@@ -273,15 +310,15 @@ def tile_gemma3naudiorelativepositionembedding_pa_t_kernel(tc, queries, keys, si
             k_mx[i] = (k_codes, k_scales)
 
         def content(i, t):
-            q_codes, q_scales = q_mx[i]
+            q_codes, q_scales = q_mx[i // 2]
             k_codes, k_scales = k_mx[i]
             acc = psum.tile([P, C], F32, tag="bd" if i == NBLK - 1 else "ac", bufs=2, name="acc")
             for g in range(2):
-                qcol = 256 * g + 128 * t
+                qcol = 256 * (i % 2) + 128 * t
                 nc.tensor.matmul_mx(
                     out=acc[:],
-                    lhsT=q_codes[:, qcol : qcol + 128].bitcast(FP8X4),
-                    lhsT_scale=q_scales[:, qcol : qcol + 128],
+                    lhsT=q_codes[:, g, qcol : qcol + 128].bitcast(FP8X4),
+                    lhsT_scale=q_scales[:, g, qcol : qcol + 128],
                     rhs=k_codes[:, 512 * g : 512 * g + 512].bitcast(FP8X4),
                     rhs_scale=k_scales[:, 512 * g : 512 * g + 512],
                     start=(g == 0),
@@ -317,6 +354,8 @@ def tile_gemma3naudiorelativepositionembedding_pa_t_kernel(tc, queries, keys, si
                 queue.dma_start(out=o_view[stored[0]], in_=results[stored[0]][:])
                 stored[0] += 1
 
+        def store_half(i, t):
+            nc.sync.dma_start(out=o_view[i, :, t, :], in_=results[i][:, t, :])
         for s in range(-Q_AHEAD, NBLK + 2):
             j_t, j_b, i_c, i_a = s + Q_AHEAD, s + B_AHEAD, s - 1, s - 2
             has_k = 0 <= s < NBLK
@@ -330,8 +369,8 @@ def tile_gemma3naudiorelativepositionembedding_pa_t_kernel(tc, queries, keys, si
                 load_k(EARLY_K_LOADS[s])
             elif 4 <= s + K_LOAD < NBLK:
                 load_k(s + K_LOAD)
-            if Q_LOAD - Q_AHEAD <= s + Q_LOAD < NBLK:
-                load_pair_rows(s + Q_LOAD, q_view[s + Q_LOAD])
+            if 4 <= s + Q_LOAD < NBLK and (s + Q_LOAD) % 2 == 0:
+                load_q((s + Q_LOAD) // 2)
             store_up_to(i_a - STORE_LAG if s + K_LOAD < NBLK else i_a - 1, nc.sync)
             if pair_due(WRITE_LAG) is not None:
                 park_write(pair_due(WRITE_LAG))
@@ -340,12 +379,14 @@ def tile_gemma3naudiorelativepositionembedding_pa_t_kernel(tc, queries, keys, si
             if pair_due(MASK_LAG) is not None:
                 mask(pair_due(MASK_LAG))
             if 0 <= j_t - 1 < NBLK:
-                quantise_q(j_t - 1)
+                quantise_q((j_t - 1) // 2, (j_t - 1) % 2)
             if 0 <= i_a:
-                add_up(i_a, 0)
-                add_up(i_a, 1)
+                for t in range(2):
+                    add_up(i_a, t)
+                    if i_a == NBLK - 1:
+                        store_half(i_a, t)
             if Q_SORT_FROM <= j_t + SORT_LEAD < NBLK:
-                sort_pair_rows(j_t + SORT_LEAD, nc.vector, F32)
+                sort_q((j_t + SORT_LEAD) // 2, (j_t + SORT_LEAD) % 2, nc.vector, F32)
             if K_SORT_FROM < 4 and 0 <= s + SORT_LEAD < NBLK:
                 sort_k(s + SORT_LEAD, nc.vector, F32)
             if has_k:
@@ -357,7 +398,7 @@ def tile_gemma3naudiorelativepositionembedding_pa_t_kernel(tc, queries, keys, si
             if has_k:
                 transpose_k(s, (2, 3))
             if j_t < NBLK:
-                transpose_pair_rows(j_t, True, (0, 0) if has_k else (0, 1))
+                transpose_q(j_t // 2, j_t % 2, (0, 0) if has_k else (0, 1))
             if s == -Q_AHEAD:
                 project()
             if has_k:
@@ -371,4 +412,3 @@ def tile_gemma3naudiorelativepositionembedding_pa_t_kernel(tc, queries, keys, si
                 content(i_c, 1)
                 copy_rest(i_c, 0)
                 copy_rest(i_c, 1)
-        store_up_to(NBLK - 1, nc.sync)

from contextlib import ExitStack

import concourse.mybir as mybir
from concourse.masks import make_identity

F32 = mybir.dt.float32
BF16 = mybir.dt.bfloat16
U32 = mybir.dt.uint32
U8 = mybir.dt.uint8
FP8X4 = mybir.dt.float8_e4m3fn_x4
ADD = mybir.AluOpType.add
IS_GE = mybir.AluOpType.is_ge

P = 128
NBLK = 16
U = 256
C = 512
D = 1024
F = 256
PARKED = 4
RING = 2 * F * PARKED
PITCH = 128 + RING
Q_AHEAD = 9
B_AHEAD = 6
WRITE_LAG = 1
READ_LAG = 2
MASK_LAG = 4
X_BUFS = 2
PARK_BUFS = 2
K_LOAD = 2
SORT_LEAD = 1
Q_SORT_FROM = 9
W_SORT_FROM = 9
K_SORT_FROM = 3
K_ON_VECTOR = ()
Q_LOAD = Q_AHEAD + 3
STORE_LAG = 4
EARLY_K_LOADS = {-6: 0, -5: 1, -3: 2, -1: 3}

FLOPS = 2 * F * D * D + NBLK * 2 * U * D * (C + F)


def tile_gemma3naudiorelativepositionembedding_pa_t_kernel(tc, queries, keys, sin_emb, pos_w, out):
    nc = tc.nc
    q_view = queries.rearrange("b (n w) u h d -> (b n) (w u) (h d)", w=2).rearrange("n (p e) d -> n p (e d)", e=4)
    k_view = keys.rearrange("b w (p t) h d -> (b w) p (t h d)", t=4)
    s_view = sin_emb.rearrange("(p e) i -> p (e i)", e=2)
    w_view = pos_w.rearrange("(g p t) i -> g p (t i)", g=2, t=4)
    o_view = out.rearrange("b h w (t p) c -> (b h w) p t c", t=2)
    o_flat = out.rearrange("(b e) h w u c -> (b e h w u c)", e=1)

    with ExitStack() as ctx:
        const = ctx.enter_context(tc.tile_pool(name="const", bufs=1))
        raws = ctx.enter_context(tc.tile_pool(name="raws", bufs=6))
        work = ctx.enter_context(tc.tile_pool(name="work", bufs=2))
        keep = ctx.enter_context(tc.tile_pool(name="keep", bufs=Q_AHEAD // 2 + 2))
        psum = ctx.enter_context(tc.psum_pool(name="psum", bufs=2))
        ctx.enter_context(tc.manual_schedule())

        pair_raw = {}
        pair_sorted = {}
        q_raw = {}
        q_sorted = {}
        q_grouped = {}
        k_raw = {}
        k_sorted = {}
        pair_grouped = {}
        q_mx = {}
        k_grouped = {}
        k_mx = {}
        accs = {}
        bds = {}
        parks = {}
        shifted = {}
        results = {}

        def load_pair_rows(key, src):
            raw = raws.tile([P, 4 * D], BF16, tag="q4raw", bufs=4)
            nc.sync.dma_start(out=raw[:, 0 : 2 * D], in_=src)
            pair_raw[key] = raw[:, 0 : 2 * D]

        def load_k(i):
            raw = raws.tile([P, 4 * D], BF16, tag="kraw", bufs=4)
            nc.sync.dma_start(out=raw[:], in_=k_view[i])
            k_raw[i] = raw

        def load_q(n):
            raw = raws.tile([P, 4 * D], BF16, tag="q4raw", bufs=4)
            nc.sync.dma_start(out=raw[:], in_=q_view[n])
            q_raw[n] = raw

        load_pair_rows("s", s_view)
        for g in range(2):
            raw = raws.tile([P, 4 * D], BF16, tag="q4raw", bufs=4, name="w_raw")
            nc.sync.dma_start(out=raw[:], in_=w_view[g])
            for h in range(2):
                pair_raw["w%d" % (2 * g + h)] = raw[:, 2 * D * h : 2 * D * h + 2 * D]
        for n in range(2):
            load_q(n)

        ident = const.tile([P, P], F32, name="ident")
        make_identity(nc, ident[:])
        lows = []
        for n in range(X_BUFS):
            low = const.tile([P, 2 * PARKED, 128], F32, name="low%d" % n)
            lows.append(low)

        def copy_out(engine, dst, src):
            if engine == 0:
                nc.scalar.copy(out=dst, in_=src)
            else:
                nc.vector.tensor_copy(out=dst, in_=src)

        def sort_words(engine, dst, src, dtype):
            engine.tensor_copy(
                out=dst.bitcast(dtype).rearrange("p (q u m) -> p q u m", u=2, m=128),
                in_=src.bitcast(dtype).rearrange("p (q m u) -> p q u m", u=2, m=128),
            )

        def sort_pair_rows(key, engine, dtype):
            dst = work.tile([P, 2 * D], BF16, tag="qs", bufs=3)
            sort_words(engine, dst[:], pair_raw[key], dtype)
            pair_sorted[key] = dst[:]

        def sort_k(i, engine, dtype):
            dst = work.tile([P, (4 - K_SORT_FROM) * D], BF16, tag="ks")
            sort_words(engine, dst[:], k_raw[i][:, K_SORT_FROM * D :], dtype)
            k_sorted[i] = dst

        def transpose_pair_rows(key, natural, engines):
            ordered = key in pair_sorted
            words = (pair_sorted[key] if ordered else pair_raw[key]).bitcast(F32)
            grouped = work.tile([P, 2 * U * 4], BF16, tag="qg", bufs=3, align_bytes=64)
            g32 = grouped[:].bitcast(F32).rearrange("p (g c u) -> p g c u", g=2, u=2)
            for g in range(2):
                bank = psum.tile([P, 4, P], F32, tag="tp", bufs=4)
                for e in range(2):
                    for u2 in range(2):
                        col = 512 * e + 256 * g
                        if ordered:
                            src = words[:, col + 128 * u2 : col + 128 * u2 + 128]
                        else:
                            src = words[:, col + u2 : col + 256 : 2]
                        nc.tensor.transpose(bank[:, 2 * e + u2, :], src, ident[:])
                if natural:
                    dst = g32[:, g].rearrange("p (r e) u -> p r e u", e=2)
                    bsrc = bank[:].rearrange("p (e u) r -> p r e u", e=2)
                else:
                    dst = g32[:, g].rearrange("p (e r) u -> p e r u", e=2)
                    bsrc = bank[:].rearrange("p (e u) r -> p e r u", e=2)
                copy_out(engines[g], dst, bsrc)
            pair_grouped[key] = grouped

        def sort_q(n, g, engine, dtype):
            dst = work.tile([P, 2 * D], BF16, tag="qs", bufs=3)
            src = q_raw[n][:].bitcast(dtype).rearrange("p (e g m u) -> p g e u m", e=4, g=2, u=2)[:, g]
            engine.tensor_copy(out=dst[:].bitcast(dtype).rearrange("p (e u m) -> p e u m", e=4, u=2), in_=src)
            q_sorted[(n, g)] = dst

        def transpose_q(n, g, engines):
            grouped = work.tile([P, 2 * U * 4], BF16, tag="qg", bufs=3, align_bytes=64)
            g32 = grouped[:].bitcast(F32).rearrange("p (b r e u) -> p b r e u", b=2, e=4, u=2)
            ordered = (n, g) in q_sorted
            for eh in range(2):
                bank = psum.tile([P, 4, P], F32, tag="tp", bufs=4)
                for k in range(4):
                    e, u2 = 2 * eh + k // 2, k % 2
                    if ordered:
                        src = q_sorted[(n, g)][:].bitcast(F32)[:, 256 * e + 128 * u2 : 256 * e + 128 * u2 + 128]
                    else:
                        col = 512 * e + 256 * g
                        src = q_raw[n][:].bitcast(F32)[:, col + u2 : col + 256 : 2]
                    nc.tensor.transpose(bank[:, k, :], src, ident[:])
                for_b = bank[:].rearrange("p (e u) (b r) -> p b r e u", e=2, b=2)
                copy_out(engines[eh], g32[:, :, :, 2 * eh : 2 * eh + 2, :], for_b)
            q_grouped[(n, g)] = grouped

        def quantise_pair_rows(key, codes, scales):
            nc.vector.quantize_mx(out=codes.bitcast(FP8X4), scales=scales, in_=pair_grouped[key][:])

        s_codes = const.tile([P, 2 * F], U32, name="s_codes", align_bytes=64)
        s_scales = const.tile([P, 2 * F], U8, name="s_scales", align_bytes=64)
        w_codes = work.tile([P, 4, 512], U32, tag="kg", align_bytes=64, name="w_codes")
        w_scales = const.tile([P, 4, 512], U8, name="w_scales", align_bytes=64)
        p_grouped = work.tile([P, 2 * F * 4], BF16, tag="kg", align_bytes=64, name="p_grouped")
        pg = p_grouped[:].rearrange("p (g f t) -> p g f t", g=2, t=4)
        p_codes = const.tile([P, 2 * F], U32, name="p_codes", align_bytes=64)
        p_scales = const.tile([P, 2 * F], U8, name="p_scales", align_bytes=64)

        transpose_pair_rows("s", True, (0, 1))
        transpose_pair_rows("w0", False, (0, 1))
        quantise_pair_rows("s", s_codes[:], s_scales[:])
        for h in range(1, 4):
            transpose_pair_rows("w%d" % h, False, (0, 1))
            quantise_pair_rows("w%d" % (h - 1), w_codes[:, h - 1, :], w_scales[:, h - 1, :])

        def project():
            quantise_pair_rows("w3", w_codes[:, 3, :], w_scales[:, 3, :])
            for g in range(2):
                for fh in range(2):
                    pb = psum.tile([P, 4, 128], F32, tag="bd", bufs=2)
                    for t in range(4):
                        h = 2 * g + t // 2
                        e = t % 2
                        for gi in range(2):
                            wcol = 256 * gi + 128 * e
                            scol = 256 * gi + 128 * fh
                            nc.tensor.matmul_mx(
                                out=pb[:, t, :],
                                lhsT=w_codes[:, h, wcol : wcol + 128].bitcast(FP8X4),
                                lhsT_scale=w_scales[:, h, wcol : wcol + 128],
                                rhs=s_codes[:, scol : scol + 128].bitcast(FP8X4),
                                rhs_scale=s_scales[:, scol : scol + 128],
                                start=(gi == 0),
                                stop=(gi == 1),
                            )
                    copy_out(fh, pg[:, g, 128 * fh : 128 * fh + 128, :], pb[:].rearrange("p t f -> p f t"))
            nc.vector.quantize_mx(out=p_codes[:].bitcast(FP8X4), scales=p_scales[:], in_=p_grouped[:])

        def quantise_q(n, g):
            if g == 0:
                q_codes = keep.tile([P, 2, 2 * U], U32, tag="q_codes", align_bytes=64)
                q_scales = keep.tile([P, 2, 2 * U], U8, tag="q_scales", align_bytes=64)
                q_mx[n] = (q_codes, q_scales)
            q_codes, q_scales = q_mx[n]
            nc.vector.quantize_mx(out=q_codes[:, g, :].bitcast(FP8X4), scales=q_scales[:, g, :], in_=q_grouped[(n, g)][:])

        def positions(j, t):
            q_codes, q_scales = q_mx[j // 2]
            if t == 0:
                bds[j] = psum.tile([P, 2, F], F32, tag="bd", bufs=2, name="bd")
            bd = bds[j]
            for g in range(2):
                qcol = 256 * (j % 2) + 128 * t
                nc.tensor.matmul_mx(
                    out=bd[:, t, :],
                    lhsT=q_codes[:, g, qcol : qcol + 128].bitcast(FP8X4),
                    lhsT_scale=q_scales[:, g, qcol : qcol + 128],
                    rhs=p_codes[:, 256 * g : 256 * g + 256].bitcast(FP8X4),
                    rhs_scale=p_scales[:, 256 * g : 256 * g + 256],
                    start=(g == 0),
                    stop=(g == 1),
                )

        def park_rows(j):
            bd = bds[j]
            b = j % PARKED
            if b == 0:
                parks[j // PARKED] = work.tile([P, PITCH], F32, tag="park", bufs=PARK_BUFS, name="park")
            park = parks[j // PARKED]
            nc.scalar.copy(out=park[:, 128 + 512 * b : 640 + 512 * b], in_=bd[:].rearrange("p t f -> p (t f)"))
            if b == PARKED - 1:
                nc.scalar.copy(out=park[:, 0:128], in_=bd[:, 1, 128:256])

        def park_write(n):
            base = n * PARKED * U * C
            nc.sync.dma_start(
                out=o_flat[base : base + P * PITCH].rearrange("(p s) -> p s", s=PITCH), in_=parks[n][:]
            )

        def read_back(n):
            base = n * PARKED * U * C + 128
            x = keep.tile([P, 4 * PARKED, 128], F32, tag="x", bufs=X_BUFS)
            nc.sync.dma_start(
                out=x[:].rearrange("p s j -> p (s j)"),
                in_=o_flat[base : base + P * (PITCH - 1)].rearrange("(p s) -> p s", s=PITCH - 1)[:, 0:RING],
            )
            shifted[n] = x

        def mask(n):
            x, low = shifted[n], lows[n % X_BUFS]
            for tile in range(2 * PARKED):
                before = (tile - 1) % (2 * PARKED)
                shared = x[:, 2 * tile, :]
                nc.gpsimd.affine_select(
                    out=low[:, before, :], in_=shared, pattern=[[-1, 128]],
                    compare_op=IS_GE, fill=0.0, base=-1, channel_multiplier=1,
                )
                nc.gpsimd.affine_select(
                    out=shared, in_=shared, pattern=[[1, 128]],
                    compare_op=IS_GE, fill=0.0, base=0, channel_multiplier=-1,
                )

        def transpose_k(i, banks):
            words = k_raw[i][:].bitcast(F32)
            if banks[0] == 0:
                k_grouped[i] = work.tile([P, 2 * C * 4], BF16, tag="kg", align_bytes=64, name="kg")
            grouped = k_grouped[i]
            g32 = grouped[:].bitcast(F32).rearrange("p (g n u) -> p g n u", g=2, u=2)
            for tt in banks:
                bank = psum.tile([P, 4, P], F32, tag="tp", bufs=4)
                for w in range(4):
                    if tt >= K_SORT_FROM:
                        col = 512 * (tt - K_SORT_FROM) + 128 * w
                        src = k_sorted[i][:].bitcast(F32)[:, col : col + 128]
                    else:
                        col = 512 * tt + 256 * (w // 2)
                        src = words[:, col + w % 2 : col + 256 : 2]
                    nc.tensor.transpose(bank[:, w, :], src, ident[:])
                copy_out(
                    1 if tt in K_ON_VECTOR else 0,
                    g32[:, :, 128 * tt : 128 * tt + 128, :],
                    bank[:].rearrange("p (g u) r -> p g r u", g=2),
                )

        def quantise_k(i):
            k_codes = work.tile([P, 2 * C], U32, tag="k_codes", align_bytes=64)
            k_scales = work.tile([P, 2 * C], U8, tag="k_scales", align_bytes=64)
            nc.vector.quantize_mx(out=k_codes[:].bitcast(FP8X4), scales=k_scales[:], in_=k_grouped[i][:])
            k_mx[i] = (k_codes, k_scales)

        def content(i, t):
            q_codes, q_scales = q_mx[i // 2]
            k_codes, k_scales = k_mx[i]
            acc = psum.tile([P, C], F32, tag="bd" if i == NBLK - 1 else "ac", bufs=2, name="acc")
            for g in range(2):
                qcol = 256 * (i % 2) + 128 * t
                nc.tensor.matmul_mx(
                    out=acc[:],
                    lhsT=q_codes[:, g, qcol : qcol + 128].bitcast(FP8X4),
                    lhsT_scale=q_scales[:, g, qcol : qcol + 128],
                    rhs=k_codes[:, 512 * g : 512 * g + 512].bitcast(FP8X4),
                    rhs_scale=k_scales[:, 512 * g : 512 * g + 512],
                    start=(g == 0),
                    stop=(g == 1),
                )
            accs[(i, t)] = acc

        def segments(i, t):
            return (
                accs[(i, t)][:].rearrange("p (tt s r) -> p s r tt", tt=4, s=4),
                results[i][:, t, :].rearrange("p (s r tt) -> p s r tt", s=4, tt=4),
            )

        def copy_rest(i, t):
            if t == 0:
                results[i] = work.tile([P, 2, C], F32, tag="res", bufs=STORE_LAG + 3, name="res")
            a_seg, o_seg = segments(i, t)
            rest = 3 - 3 * t
            nc.scalar.copy(out=o_seg[:, rest : rest + 1], in_=a_seg[:, rest : rest + 1])

        def add_up(i, t):
            n, b = divmod(i, PARKED)
            x_seg = shifted[n][:, 4 * b + 2 * t : 4 * b + 2 * t + 2, :].rearrange("p s (r tt) -> p s r tt", tt=4)
            l_seg = lows[n % X_BUFS][:, 2 * b + t : 2 * b + t + 1, :].rearrange("p s (r tt) -> p s r tt", tt=4)
            a_seg, o_seg = segments(i, t)
            nc.vector.tensor_tensor(out=o_seg[:, t : t + 2], in0=a_seg[:, t : t + 2], in1=x_seg, op=ADD)
            nc.vector.tensor_tensor(out=o_seg[:, t + 2 : t + 3], in0=a_seg[:, t + 2 : t + 3], in1=l_seg, op=ADD)

        stored = [0]

        def store_up_to(last, queue):
            while stored[0] <= last:
                queue.dma_start(out=o_view[stored[0]], in_=results[stored[0]][:])
                stored[0] += 1

        def store_half(i, t):
            nc.sync.dma_start(out=o_view[i, :, t, :], in_=results[i][:, t, :])
        for s in range(-Q_AHEAD, NBLK + 2):
            j_t, j_b, i_c, i_a = s + Q_AHEAD, s + B_AHEAD, s - 1, s - 2
            has_k = 0 <= s < NBLK
            has_b = 0 <= j_b < NBLK

            def pair_due(lag):
                j = s + B_AHEAD - lag
                return j // PARKED if PARKED - 1 <= j < NBLK and j % PARKED == PARKED - 1 else None

            if s in EARLY_K_LOADS:
                load_k(EARLY_K_LOADS[s])
            elif 4 <= s + K_LOAD < NBLK:
                load_k(s + K_LOAD)
            if 4 <= s + Q_LOAD < NBLK and (s + Q_LOAD) % 2 == 0:
                load_q((s + Q_LOAD) // 2)
            store_up_to(i_a - STORE_LAG if s + K_LOAD < NBLK else i_a - 1, nc.sync)
            if pair_due(WRITE_LAG) is not None:
                park_write(pair_due(WRITE_LAG))
            if pair_due(READ_LAG) is not None:
                read_back(pair_due(READ_LAG))
            if pair_due(MASK_LAG) is not None:
                mask(pair_due(MASK_LAG))
            if 0 <= j_t - 1 < NBLK:
                quantise_q((j_t - 1) // 2, (j_t - 1) % 2)
            if 0 <= i_a:
                for t in range(2):
                    add_up(i_a, t)
                    if i_a == NBLK - 1:
                        store_half(i_a, t)
            if Q_SORT_FROM <= j_t + SORT_LEAD < NBLK:
                sort_q((j_t + SORT_LEAD) // 2, (j_t + SORT_LEAD) % 2, nc.vector, F32)
            if K_SORT_FROM < 4 and 0 <= s + SORT_LEAD < NBLK:
                sort_k(s + SORT_LEAD, nc.vector, F32)
            if has_k:
                transpose_k(s, (0, 1))
            if has_b and has_k:
                positions(j_b, 0)
                positions(j_b, 1)
                park_rows(j_b)
            if has_k:
                transpose_k(s, (2, 3))
            if j_t < NBLK:
                transpose_q(j_t // 2, j_t % 2, (0, 0) if has_k else (0, 1))
            if s == -Q_AHEAD:
                project()
            if has_k:
                quantise_k(s)
            if has_b and not has_k:
                positions(j_b, 0)
                positions(j_b, 1)
                park_rows(j_b)
            if 0 <= i_c < NBLK:
                content(i_c, 0)
                content(i_c, 1)
                copy_rest(i_c, 0)
                copy_rest(i_c, 1)
